import numpy as np
import ml_dtypes


def mxq(x, axis, fmt="e4m3"):
    dtype, down = {"e4m3": (ml_dtypes.float8_e4m3fn, 7), "e5m2": (ml_dtypes.float8_e5m2, 14)}[fmt]
    v = np.moveaxis(np.asarray(x, np.float32).astype(ml_dtypes.bfloat16).astype(np.float64), axis, -1)
    blocks = v.reshape(v.shape[:-1] + (-1, 32))
    amax = np.abs(blocks).max(-1, keepdims=True)
    byte = np.maximum(np.where(amax > 0, np.frexp(amax)[1] - 1 + 127, 0) - down, 1)
    scale = np.exp2(byte - 127.0)
    codes = (blocks / scale).astype(np.float32).astype(dtype).astype(np.float64)
    return np.moveaxis((codes * scale).reshape(v.shape), -1, axis)


WIDE = False


def mx_kscale(k):
    if not WIDE:
        return np.ones(k)
    levels = np.array([10, -10, 5, -5, 0])
    a = np.random.permutation(np.resize(levels, k // 512 * 4)).reshape(k // 512, 4)
    idx = np.arange(k)
    return np.exp2(a[idx // 512, idx % 128 // 32])


BF16 = ml_dtypes.bfloat16


def bf(x):
    return np.asarray(x, np.float32).astype(BF16)


def f64(x):
    return np.asarray(x).astype(np.float64)


E2M1 = np.array([0.0, 0.5, 1.0, 1.5, 2.0, 3.0, 4.0, 6.0, -0.0, -0.5, -1.0, -1.5, -2.0, -3.0, -4.0, -6.0])


def pack_weight(w, fmt):
    k, n = w.shape
    w = f64(bf(w)).reshape(k // 32, 32, n)
    amax = np.abs(w).max(1)
    if fmt == "e4m3":
        byte = np.frexp(amax)[1] - 1 + 127 - 7
    else:
        mant, ex = np.frexp(amax / 6.0)
        byte = np.where(mant > 0.5, ex, ex - 1) + 127
    byte = np.clip(np.where(amax > 0, byte, 1), 1, 254)
    scaled = (w * np.exp2(127.0 - byte)[:, None, :]).reshape(k, n).astype(np.float32)
    by_word = np.ascontiguousarray(scaled.reshape(k // 512, 128, 4, n).transpose(0, 1, 3, 2))
    if fmt == "e4m3":
        words = by_word.astype(ml_dtypes.float8_e4m3fn).view(np.uint8)
    else:
        c = by_word.astype(ml_dtypes.float4_e2m1fn).view(np.uint8) & 0xF
        words = c[..., 0::2] | (c[..., 1::2] << 4)
    return np.ascontiguousarray(words), np.ascontiguousarray(byte.astype(np.uint8).reshape(k // 512, 16, n))


def unpack_weight(words, scales, fmt):
    g, p, n, _ = words.shape
    if fmt == "e4m3":
        vals = np.ascontiguousarray(words).view(ml_dtypes.float8_e4m3fn).astype(np.float64)
    else:
        nib = np.empty((g, p, n, 4), np.uint8)
        nib[..., 0::2] = words & 0xF
        nib[..., 1::2] = words >> 4
        vals = E2M1[nib]
    vals = vals * np.repeat(np.exp2(scales.astype(np.float64) - 127.0), 8, axis=1)[..., None]
    return vals.transpose(0, 1, 3, 2).reshape(g * 512, n)


B, C, K, L, R = 4, 64, 1024, 4, 128
FMT = "e4m3"


def transition():
    g = np.exp(2.5 * np.random.standard_normal((K, K)))
    return g / g.sum(1, keepdims=True)


def setup_inputs():
    s = mx_kscale(K)
    x = np.random.standard_normal((B, C, K, L)) * 2.0 * s[None, None, :, None]
    words0, scales0 = pack_weight((transition() * s[:, None] / s[None, :]).T, FMT)
    words1, scales1 = pack_weight((transition() * s[:, None] / s[None, :]).T, FMT)
    return {'x': bf(x.reshape(B, C, K * L)),
            'support0_words': words0, 'support0_scales': scales0,
            'support1_words': words1, 'support1_scales': scales1}


def two_hops(xq, aq):
    x1 = xq @ aq
    x2 = mxq(x1, 2, 'e4m3') @ aq
    return x1, x2


def reference(x, support0_words, support0_scales, support1_words, support1_scales):
    xr = f64(x).reshape(B, C, K, L).transpose(0, 3, 1, 2).reshape(B * L, C, K)
    xq = mxq(xr, 2, 'e4m3')
    f1, f2 = two_hops(xq, unpack_weight(support0_words, support0_scales, FMT))
    g1, g2 = two_hops(xq, unpack_weight(support1_words, support1_scales, FMT))
    return f1, f2, g1, g2

@@ -1,0 +1,224 @@
+from contextlib import ExitStack
+
+import concourse.mybir as mybir
+from concourse.masks import make_identity
+
+F32 = mybir.dt.float32
+BF16 = mybir.dt.bfloat16
+I32 = mybir.dt.int32
+U32 = mybir.dt.uint32
+U8 = mybir.dt.uint8
+FP8X4 = mybir.dt.float8_e4m3fn_x4
+
+P = 128
+NODES = 1024
+GROUPS = 2
+BANK = 512
+HALVES = NODES // BANK
+BLOCKS = 4
+TILES = 2
+STEPS = 4
+SUPPORTS = 2
+TILE_WORDS = GROUPS * P
+
+FLOPS = 2 * 2 * SUPPORTS * 1024 * NODES * NODES
+
+
+def tile_adaptivegcn_pb_kernel(
+    tc,
+    x,
+    support0_words,
+    support0_scales,
+    support1_words,
+    support1_scales,
+    out_0,
+    out_1,
+    out_2,
+    out_3,
+):
+    nc = tc.nc
+    words_in = [support0_words, support1_words]
+    scales_in = [support0_scales, support1_scales]
+    hop1_out = [out_0.flatten_outer_dims(), out_2.flatten_outer_dims()]
+    hop2_out = [out_1.flatten_outer_dims(), out_3.flatten_outer_dims()]
+
+    with ExitStack() as ctx:
+        ctx.enter_context(tc.manual_schedule())
+        keep = ctx.enter_context(tc.tile_pool(name="keep", bufs=1))
+        grouped_pool = ctx.enter_context(tc.tile_pool(name="grouped", bufs=6))
+        hop1_q_pool = ctx.enter_context(tc.tile_pool(name="hop1_q", bufs=8))
+        hop1_bf_pool = ctx.enter_context(tc.tile_pool(name="hop1_bf", bufs=8))
+        result_pool = ctx.enter_context(tc.tile_pool(name="result", bufs=12))
+        sum_pool = ctx.enter_context(tc.psum_pool(name="sums", bufs=4))
+        flip_pool = ctx.enter_context(tc.psum_pool(name="flips", bufs=4))
+
+        identity = keep.tile([P, P], F32)
+        make_identity(nc, identity[:])
+
+        x_raw = keep.tile([P, BLOCKS, BANK * STEPS], BF16)
+        x_view = x.rearrange("b c (g f) -> b (c g) f", g=GROUPS)
+        w_words = keep.tile([P, SUPPORTS, GROUPS, NODES], U32, align_bytes=64)
+        w_scales = keep.tile([P, NODES], U8, align_bytes=64)
+        nc.vector.memset(w_scales[:].bitcast(I32), 0)
+
+        def load_x(b):
+            nc.sync.dma_start(out=x_raw[:, b, :], in_=x_view[b])
+
+        def load_support(s):
+            for quadrant in range(4):
+                first = 32 * quadrant + 8 * s
+                nc.sync.dma_start(
+                    out=w_scales[first : first + 8, :].bitcast(I32),
+                    in_=scales_in[s][:, 4 * quadrant : 4 * quadrant + 4, :].bitcast(I32),
+                )
+            for g in range(GROUPS):
+                nc.sync.dma_start(
+                    out=w_words[:, s, g, :].bitcast(I32),
+                    in_=words_in[s][g].rearrange("p n t -> p (n t)").bitcast(I32),
+                )
+
+        load_x(0)
+        load_x(1)
+        load_support(0)
+        load_support(1)
+        load_x(2)
+        load_x(3)
+
+        x_sorted = keep.tile([P, BLOCKS, STEPS * BANK], BF16)
+        x_codes = keep.tile([P, BLOCKS * TILES, TILE_WORDS], U32, align_bytes=64)
+        x_scales = keep.tile([P, BLOCKS * TILES, TILE_WORDS], U8, align_bytes=64)
+
+        def sort_x(b):
+            by_step = x_raw[:, b, :].rearrange("q (p u e l) -> q l u p e", u=2, e=2, l=STEPS)
+            for step in range(STEPS):
+                copy = nc.vector.tensor_copy if step < STEPS // TILES else nc.scalar.copy
+                copy(
+                    out=x_sorted[:, b, step * BANK : (step + 1) * BANK].rearrange(
+                        "q (u p e) -> q u p e", u=2, e=2
+                    ),
+                    in_=by_step[:, step],
+                )
+
+        def flip_x(b, tile_in_block):
+            flipped = flip_pool.tile([P, BANK], F32, name="flipped")
+            planes = x_sorted[:, b, :].bitcast(F32)
+            for plane in range(4):
+                source = 4 * tile_in_block + plane
+                nc.tensor.transpose(
+                    flipped[:, plane * P : (plane + 1) * P],
+                    planes[:, source * P : (source + 1) * P],
+                    identity[:],
+                )
+            return flipped
+
+        def group_x(flipped):
+            grouped = grouped_pool.tile([P, 4 * TILE_WORDS], BF16, name="grouped", align_bytes=64)
+            by_group = flipped[:].rearrange("p (l u c g) -> p g l c u", l=2, u=2, g=GROUPS)
+            pairs = grouped[:].bitcast(F32).rearrange("p (g l c u) -> p g l c u", g=GROUPS, l=2, u=2)
+            for g in range(GROUPS):
+                nc.vector.tensor_copy(out=pairs[:, g], in_=by_group[:, g])
+            return grouped
+
+        def hop(codes, scales, s, out_rows, sorted_bf16):
+            result = result_pool.tile([P, NODES], F32, name="result")
+            for half in range(HALVES):
+                columns = slice(half * BANK, (half + 1) * BANK)
+                sums = sum_pool.tile([P, BANK], F32, name="sums")
+                for g in range(GROUPS):
+                    rows = slice(g * P, (g + 1) * P)
+                    nc.tensor.matmul_mx(
+                        out=sums[:],
+                        lhsT=codes[:, rows].bitcast(FP8X4),
+                        lhsT_scale=scales[:, rows],
+                        rhs=w_words[:, s, g, columns].bitcast(FP8X4),
+                        rhs_scale=w_scales[8 * s + 4 * g : P, columns],
+                        start=(g == 0),
+                        stop=(g == GROUPS - 1),
+                    )
+                nc.scalar.copy(out=result[:, columns], in_=sums[:])
+                if sorted_bf16 is not None:
+                    nc.vector.tensor_copy(
+                        out=sorted_bf16[:, columns].rearrange("m (u p e) -> m u p e", u=2, e=2),
+                        in_=result[:, columns].rearrange("m (p u e) -> m u p e", u=2, e=2),
+                    )
+            nc.sync.dma_start(out=out_rows, in_=result[:])
+
+        def flip_hop1(sorted_bf16):
+            flipped = flip_pool.tile([P, BANK], F32, name="flipped")
+            planes = sorted_bf16[:].bitcast(F32)
+            for plane in range(4):
+                columns = slice(plane * P, (plane + 1) * P)
+                nc.tensor.transpose(flipped[:, columns], planes[:, columns], identity[:])
+            return flipped
+
+        def group_hop1(flipped):
+            grouped = grouped_pool.tile([P, 4 * TILE_WORDS], BF16, name="grouped", align_bytes=64)
+            nc.vector.tensor_copy(
+                out=grouped[:].bitcast(F32).rearrange("p (g m u) -> p g m u", g=GROUPS, u=2),
+                in_=flipped[:].rearrange("p (g u m) -> p g m u", g=GROUPS, u=2),
+            )
+            return grouped
+
+        def quantise(grouped, codes, scales):
+            nc.vector.quantize_mx(out=codes.bitcast(FP8X4), scales=scales, in_=grouped[:])
+
+        hop1_bf = {}
+
+        def first_hop(block, s):
+            for t in range(TILES):
+                row_tile = block * TILES + t
+                sorted_bf16 = hop1_bf_pool.tile([P, NODES], BF16, name="sorted_bf16")
+                hop1_bf[(block, s, t)] = sorted_bf16
+                hop(
+                    x_codes[:, row_tile, :],
+                    x_scales[:, row_tile, :],
+                    s,
+                    hop1_out[s][row_tile * P : (row_tile + 1) * P, :],
+                    sorted_bf16,
+                )
+
+        sort_x(0)
+        for i in range(BLOCKS + 2):
+            a_block, b_block, cd_block = i, i - 1, i - 2
+            do_a = a_block < BLOCKS
+            do_b = 0 <= b_block < BLOCKS
+            do_cd = 0 <= cd_block < BLOCKS
+
+            grouped_x = []
+            if do_a:
+                for t in range(TILES):
+                    grouped_x.append(group_x(flip_x(a_block, t)))
+            grouped_h = []
+            if do_cd:
+                for s in range(SUPPORTS):
+                    for t in range(TILES):
+                        grouped_h.append(group_hop1(flip_hop1(hop1_bf[(cd_block, s, t)])))
+
+            for t, grouped in enumerate(grouped_x):
+                row_tile = a_block * TILES + t
+                quantise(grouped, x_codes[:, row_tile, :], x_scales[:, row_tile, :])
+            hop1_q = []
+            for grouped in grouped_h:
+                codes = hop1_q_pool.tile([P, TILE_WORDS], U32, name="codes", align_bytes=64)
+                scales = hop1_q_pool.tile([P, TILE_WORDS], U8, name="scales", align_bytes=64)
+                quantise(grouped, codes[:], scales[:])
+                hop1_q.append((codes, scales))
+
+            if do_b:
+                first_hop(b_block, 0)
+            if a_block + 1 < BLOCKS:
+                sort_x(a_block + 1)
+            if do_b:
+                first_hop(b_block, 1)
+            if do_cd:
+                for s in range(SUPPORTS):
+                    for t in range(TILES):
+                        row_tile = cd_block * TILES + t
+                        codes, scales = hop1_q[s * TILES + t]
+                        hop(
+                            codes[:],
+                            scales[:],
+                            s,
+                            hop2_out[s][row_tile * P : (row_tile + 1) * P, :],
+                            None,
+                        )

@@ -17,9 +17,12 @@ BANK = 512
 HALVES = NODES // BANK
 BLOCKS = 4
 TILES = 2
-STEPS = 4
+ROW_TILES = BLOCKS * TILES
+STEPS_OF_TIME = 4
 SUPPORTS = 2
 TILE_WORDS = GROUPS * P
+TILE_VALUES = 4 * TILE_WORDS
+PRODUCTS = BLOCKS * SUPPORTS
 
 FLOPS = 2 * 2 * SUPPORTS * 1024 * NODES * NODES
 
@@ -45,17 +48,17 @@ def tile_adaptivegcn_pb_kernel(
     with ExitStack() as ctx:
         ctx.enter_context(tc.manual_schedule())
         keep = ctx.enter_context(tc.tile_pool(name="keep", bufs=1))
-        grouped_pool = ctx.enter_context(tc.tile_pool(name="grouped", bufs=6))
-        hop1_q_pool = ctx.enter_context(tc.tile_pool(name="hop1_q", bufs=8))
-        hop1_bf_pool = ctx.enter_context(tc.tile_pool(name="hop1_bf", bufs=8))
+        grouped_pool = ctx.enter_context(tc.tile_pool(name="grouped", bufs=3))
+        hop1_q_pool = ctx.enter_context(tc.tile_pool(name="hop1_q", bufs=3))
+        hop1_bf_pool = ctx.enter_context(tc.tile_pool(name="hop1_bf", bufs=6))
         result_pool = ctx.enter_context(tc.tile_pool(name="result", bufs=12))
-        sum_pool = ctx.enter_context(tc.psum_pool(name="sums", bufs=4))
-        flip_pool = ctx.enter_context(tc.psum_pool(name="flips", bufs=4))
+        sum_pool = ctx.enter_context(tc.psum_pool(name="sums", bufs=5))
+        flip_pool = ctx.enter_context(tc.psum_pool(name="flips", bufs=3))
 
         identity = keep.tile([P, P], F32)
         make_identity(nc, identity[:])
 
-        x_raw = keep.tile([P, BLOCKS, BANK * STEPS], BF16)
+        x_raw = keep.tile([P, BLOCKS, BANK * STEPS_OF_TIME], BF16)
         x_view = x.rearrange("b c (g f) -> b (c g) f", g=GROUPS)
         w_words = keep.tile([P, SUPPORTS, GROUPS, NODES], U32, align_bytes=64)
         w_scales = keep.tile([P, NODES], U8, align_bytes=64)
@@ -78,32 +81,35 @@ def tile_adaptivegcn_pb_kernel(
                 )
 
         load_x(0)
-        load_x(1)
         load_support(0)
+        load_x(1)
         load_support(1)
         load_x(2)
         load_x(3)
 
-        x_sorted = keep.tile([P, BLOCKS, STEPS * BANK], BF16)
-        x_codes = keep.tile([P, BLOCKS * TILES, TILE_WORDS], U32, align_bytes=64)
-        x_scales = keep.tile([P, BLOCKS * TILES, TILE_WORDS], U8, align_bytes=64)
+        x_sorted = keep.tile([P, BLOCKS, STEPS_OF_TIME * BANK], BF16)
+        x_codes = keep.tile([P, ROW_TILES, TILE_WORDS], U32, align_bytes=64)
+        x_scales = keep.tile([P, ROW_TILES, TILE_WORDS], U8, align_bytes=64)
 
-        def sort_x(b):
-            by_step = x_raw[:, b, :].rearrange("q (p u e l) -> q l u p e", u=2, e=2, l=STEPS)
-            for step in range(STEPS):
-                copy = nc.vector.tensor_copy if step < STEPS // TILES else nc.scalar.copy
-                copy(
-                    out=x_sorted[:, b, step * BANK : (step + 1) * BANK].rearrange(
+        def sort_x(row_tile):
+            b, j = divmod(row_tile, TILES)
+            by_step = x_raw[:, b, :].rearrange(
+                "q (p u e l) -> q l u p e", u=2, e=2, l=STEPS_OF_TIME
+            )
+            for step_of_time in (2 * j, 2 * j + 1):
+                nc.vector.tensor_copy(
+                    out=x_sorted[:, b, step_of_time * BANK : (step_of_time + 1) * BANK].rearrange(
                         "q (u p e) -> q u p e", u=2, e=2
                     ),
-                    in_=by_step[:, step],
+                    in_=by_step[:, step_of_time],
                 )
 
-        def flip_x(b, tile_in_block):
+        def flip_x(row_tile):
+            b, j = divmod(row_tile, TILES)
             flipped = flip_pool.tile([P, BANK], F32, name="flipped")
             planes = x_sorted[:, b, :].bitcast(F32)
             for plane in range(4):
-                source = 4 * tile_in_block + plane
+                source = 4 * j + plane
                 nc.tensor.transpose(
                     flipped[:, plane * P : (plane + 1) * P],
                     planes[:, source * P : (source + 1) * P],
@@ -112,12 +118,19 @@ def tile_adaptivegcn_pb_kernel(
             return flipped
 
         def group_x(flipped):
-            grouped = grouped_pool.tile([P, 4 * TILE_WORDS], BF16, name="grouped", align_bytes=64)
+            grouped = grouped_pool.tile([P, TILE_VALUES], BF16, name="grouped_x", align_bytes=64)
             by_group = flipped[:].rearrange("p (l u c g) -> p g l c u", l=2, u=2, g=GROUPS)
             pairs = grouped[:].bitcast(F32).rearrange("p (g l c u) -> p g l c u", g=GROUPS, l=2, u=2)
             for g in range(GROUPS):
                 nc.vector.tensor_copy(out=pairs[:, g], in_=by_group[:, g])
             return grouped
+
+        def quantise_x(row_tile, grouped):
+            nc.vector.quantize_mx(
+                out=x_codes[:, row_tile, :].bitcast(FP8X4),
+                scales=x_scales[:, row_tile, :],
+                in_=grouped[:],
+            )
 
         def hop(codes, scales, s, out_rows, sorted_bf16):
             result = result_pool.tile([P, NODES], F32, name="result")
@@ -143,6 +156,30 @@ def tile_adaptivegcn_pb_kernel(
                     )
             nc.sync.dma_start(out=out_rows, in_=result[:])
 
+        hop1_bf = {}
+        hop1_q = {}
+
+        def rows_of(pair, j):
+            row_tile = (pair // SUPPORTS) * TILES + j
+            return row_tile, slice(row_tile * P, (row_tile + 1) * P)
+
+        def first_hop(pair):
+            s = pair % SUPPORTS
+            for j in range(TILES):
+                row_tile, rows = rows_of(pair, j)
+                sorted_bf16 = hop1_bf_pool.tile([P, NODES], BF16, name="sorted_bf16")
+                hop1_bf[TILES * pair + j] = sorted_bf16
+                hop(
+                    x_codes[:, row_tile, :], x_scales[:, row_tile, :], s, hop1_out[s][rows, :], sorted_bf16
+                )
+
+        def second_hop(pair):
+            s = pair % SUPPORTS
+            for j in range(TILES):
+                row_tile, rows = rows_of(pair, j)
+                codes, scales = hop1_q[TILES * pair + j]
+                hop(codes, scales, s, hop2_out[s][rows, :], None)
+
         def flip_hop1(sorted_bf16):
             flipped = flip_pool.tile([P, BANK], F32, name="flipped")
             planes = sorted_bf16[:].bitcast(F32)
@@ -151,74 +188,48 @@ def tile_adaptivegcn_pb_kernel(
                 nc.tensor.transpose(flipped[:, columns], planes[:, columns], identity[:])
             return flipped
 
-        def group_hop1(flipped):
-            grouped = grouped_pool.tile([P, 4 * TILE_WORDS], BF16, name="grouped", align_bytes=64)
+        def group_hop1(flipped, grouped):
             nc.vector.tensor_copy(
-                out=grouped[:].bitcast(F32).rearrange("p (g m u) -> p g m u", g=GROUPS, u=2),
+                out=grouped.bitcast(F32).rearrange("p (g m u) -> p g m u", g=GROUPS, u=2),
                 in_=flipped[:].rearrange("p (g u m) -> p g m u", g=GROUPS, u=2),
             )
-            return grouped
 
-        def quantise(grouped, codes, scales):
-            nc.vector.quantize_mx(out=codes.bitcast(FP8X4), scales=scales, in_=grouped[:])
+        def x_tiles_of_step(n):
+            if n < 2:
+                return [TILES * n, TILES * n + 1]
+            return [row_tile for row_tile in [n + 2] if row_tile < ROW_TILES]
 
-        hop1_bf = {}
+        for row_tile in x_tiles_of_step(0):
+            sort_x(row_tile)
+        for row_tile in x_tiles_of_step(0):
+            quantise_x(row_tile, group_x(flip_x(row_tile)))
 
-        def first_hop(block, s):
-            for t in range(TILES):
-                row_tile = block * TILES + t
-                sorted_bf16 = hop1_bf_pool.tile([P, NODES], BF16, name="sorted_bf16")
-                hop1_bf[(block, s, t)] = sorted_bf16
-                hop(
-                    x_codes[:, row_tile, :],
-                    x_scales[:, row_tile, :],
-                    s,
-                    hop1_out[s][row_tile * P : (row_tile + 1) * P, :],
-                    sorted_bf16,
+        for n in range(PRODUCTS + 2):
+            if n > 0:
+                x_tiles = x_tiles_of_step(n)
+                numbers = [r for r in (2 * n - 3, 2 * n - 2) if 0 <= r < TILES * PRODUCTS]
+                grouped_x = [group_x(flip_x(row_tile)) for row_tile in x_tiles]
+                grouped_h = grouped_pool.tile(
+                    [P, len(numbers) * TILE_VALUES], BF16, name="grouped_h", align_bytes=64
                 )
+                for place, r in enumerate(numbers):
+                    group_hop1(
+                        flip_hop1(hop1_bf[r]),
+                        grouped_h[:, place * TILE_VALUES : (place + 1) * TILE_VALUES],
+                    )
+                for row_tile, grouped in zip(x_tiles, grouped_x):
+                    quantise_x(row_tile, grouped)
+                codes = hop1_q_pool.tile([P, len(numbers) * TILE_WORDS], U32, name="codes", align_bytes=64)
+                scales = hop1_q_pool.tile([P, len(numbers) * TILE_WORDS], U8, name="scales", align_bytes=64)
+                nc.vector.quantize_mx(out=codes[:].bitcast(FP8X4), scales=scales[:], in_=grouped_h[:])
+                for place, r in enumerate(numbers):
+                    words = slice(place * TILE_WORDS, (place + 1) * TILE_WORDS)
+                    hop1_q[r] = (codes[:, words], scales[:, words])
 
-        sort_x(0)
-        for i in range(BLOCKS + 2):
-            a_block, b_block, cd_block = i, i - 1, i - 2
-            do_a = a_block < BLOCKS
-            do_b = 0 <= b_block < BLOCKS
-            do_cd = 0 <= cd_block < BLOCKS
+            for row_tile in x_tiles_of_step(n + 1):
+                sort_x(row_tile)
 
-            grouped_x = []
-            if do_a:
-                for t in range(TILES):
-                    grouped_x.append(group_x(flip_x(a_block, t)))
-            grouped_h = []
-            if do_cd:
-                for s in range(SUPPORTS):
-                    for t in range(TILES):
-                        grouped_h.append(group_hop1(flip_hop1(hop1_bf[(cd_block, s, t)])))
-
-            for t, grouped in enumerate(grouped_x):
-                row_tile = a_block * TILES + t
-                quantise(grouped, x_codes[:, row_tile, :], x_scales[:, row_tile, :])
-            hop1_q = []
-            for grouped in grouped_h:
-                codes = hop1_q_pool.tile([P, TILE_WORDS], U32, name="codes", align_bytes=64)
-                scales = hop1_q_pool.tile([P, TILE_WORDS], U8, name="scales", align_bytes=64)
-                quantise(grouped, codes[:], scales[:])
-                hop1_q.append((codes, scales))
-
-            if do_b:
-                first_hop(b_block, 0)
-            if a_block + 1 < BLOCKS:
-                sort_x(a_block + 1)
-            if do_b:
-                first_hop(b_block, 1)
-            if do_cd:
-                for s in range(SUPPORTS):
-                    for t in range(TILES):
-                        row_tile = cd_block * TILES + t
-                        codes, scales = hop1_q[s * TILES + t]
-                        hop(
-                            codes[:],
-                            scales[:],
-                            s,
-                            hop2_out[s][row_tile * P : (row_tile + 1) * P, :],
-                            None,
-                        )
+            if n < PRODUCTS:
+                first_hop(n)
+            if n >= 2:
+                second_hop(n - 2)

@@ -150,9 +150,13 @@ def tile_adaptivegcn_pb_kernel(
                     )
                 nc.scalar.copy(out=result[:, columns], in_=sums[:])
                 if sorted_bf16 is not None:
-                    nc.vector.tensor_copy(
+                    nc.gpsimd.tensor_scalar(
                         out=sorted_bf16[:, columns].rearrange("m (u p e) -> m u p e", u=2, e=2),
-                        in_=result[:, columns].rearrange("m (p u e) -> m u p e", u=2, e=2),
+                        in0=result[:, columns].rearrange("m (p u e) -> m u p e", u=2, e=2),
+                        scalar1=1.0,
+                        scalar2=0.0,
+                        op0=mybir.AluOpType.mult,
+                        op1=mybir.AluOpType.add,
                     )
             nc.sync.dma_start(out=out_rows, in_=result[:])
 

@@ -23,6 +23,7 @@ SUPPORTS = 2
 TILE_WORDS = GROUPS * P
 TILE_VALUES = 4 * TILE_WORDS
 PRODUCTS = BLOCKS * SUPPORTS
+RESULTS = TILES * PRODUCTS
 
 FLOPS = 2 * 2 * SUPPORTS * 1024 * NODES * NODES
 
@@ -48,8 +49,8 @@ def tile_adaptivegcn_pb_kernel(
     with ExitStack() as ctx:
         ctx.enter_context(tc.manual_schedule())
         keep = ctx.enter_context(tc.tile_pool(name="keep", bufs=1))
-        grouped_pool = ctx.enter_context(tc.tile_pool(name="grouped", bufs=3))
-        hop1_q_pool = ctx.enter_context(tc.tile_pool(name="hop1_q", bufs=3))
+        grouped_pool = ctx.enter_context(tc.tile_pool(name="grouped", bufs=4))
+        hop1_q_pool = ctx.enter_context(tc.tile_pool(name="hop1_q", bufs=6))
         hop1_bf_pool = ctx.enter_context(tc.tile_pool(name="hop1_bf", bufs=6))
         result_pool = ctx.enter_context(tc.tile_pool(name="result", bufs=12))
         sum_pool = ctx.enter_context(tc.psum_pool(name="sums", bufs=5))
@@ -118,47 +119,28 @@ def tile_adaptivegcn_pb_kernel(
             return flipped
 
         def group_x(flipped):
-            grouped = grouped_pool.tile([P, TILE_VALUES], BF16, name="grouped_x", align_bytes=64)
+            grouped = grouped_pool.tile([P, TILE_VALUES], BF16, name="grouped", align_bytes=64)
             by_group = flipped[:].rearrange("p (l u c g) -> p g l c u", l=2, u=2, g=GROUPS)
             pairs = grouped[:].bitcast(F32).rearrange("p (g l c u) -> p g l c u", g=GROUPS, l=2, u=2)
             for g in range(GROUPS):
                 nc.vector.tensor_copy(out=pairs[:, g], in_=by_group[:, g])
             return grouped
 
-        def quantise_x(row_tile, grouped):
-            nc.vector.quantize_mx(
-                out=x_codes[:, row_tile, :].bitcast(FP8X4),
-                scales=x_scales[:, row_tile, :],
-                in_=grouped[:],
-            )
-
-        def hop(codes, scales, s, out_rows, sorted_bf16):
-            result = result_pool.tile([P, NODES], F32, name="result")
-            for half in range(HALVES):
-                columns = slice(half * BANK, (half + 1) * BANK)
-                sums = sum_pool.tile([P, BANK], F32, name="sums")
-                for g in range(GROUPS):
-                    rows = slice(g * P, (g + 1) * P)
-                    nc.tensor.matmul_mx(
-                        out=sums[:],
-                        lhsT=codes[:, rows].bitcast(FP8X4),
-                        lhsT_scale=scales[:, rows],
-                        rhs=w_words[:, s, g, columns].bitcast(FP8X4),
-                        rhs_scale=w_scales[8 * s + 4 * g : P, columns],
-                        start=(g == 0),
-                        stop=(g == GROUPS - 1),
-                    )
-                nc.scalar.copy(out=result[:, columns], in_=sums[:])
-                if sorted_bf16 is not None:
-                    nc.gpsimd.tensor_scalar(
-                        out=sorted_bf16[:, columns].rearrange("m (u p e) -> m u p e", u=2, e=2),
-                        in0=result[:, columns].rearrange("m (p u e) -> m u p e", u=2, e=2),
-                        scalar1=1.0,
-                        scalar2=0.0,
-                        op0=mybir.AluOpType.mult,
-                        op1=mybir.AluOpType.add,
-                    )
-            nc.sync.dma_start(out=out_rows, in_=result[:])
+        def product(codes, scales, s, half):
+            columns = slice(half * BANK, (half + 1) * BANK)
+            sums = sum_pool.tile([P, BANK], F32, name="sums")
+            for g in range(GROUPS):
+                rows = slice(g * P, (g + 1) * P)
+                nc.tensor.matmul_mx(
+                    out=sums[:],
+                    lhsT=codes[:, rows].bitcast(FP8X4),
+                    lhsT_scale=scales[:, rows],
+                    rhs=w_words[:, s, g, columns].bitcast(FP8X4),
+                    rhs_scale=w_scales[8 * s + 4 * g : P, columns],
+                    start=(g == 0),
+                    stop=(g == GROUPS - 1),
+                )
+            return sums, columns
 
         hop1_bf = {}
         hop1_q = {}
@@ -171,18 +153,35 @@ def tile_adaptivegcn_pb_kernel(
             s = pair % SUPPORTS
             for j in range(TILES):
                 row_tile, rows = rows_of(pair, j)
+                result = result_pool.tile([P, NODES], F32, name="result")
                 sorted_bf16 = hop1_bf_pool.tile([P, NODES], BF16, name="sorted_bf16")
                 hop1_bf[TILES * pair + j] = sorted_bf16
-                hop(
-                    x_codes[:, row_tile, :], x_scales[:, row_tile, :], s, hop1_out[s][rows, :], sorted_bf16
-                )
+                for half in range(HALVES):
+                    sums, columns = product(x_codes[:, row_tile, :], x_scales[:, row_tile, :], s, half)
+                    nc.scalar.copy(out=result[:, columns], in_=sums[:])
+                    nc.gpsimd.tensor_scalar(
+                        out=sorted_bf16[:, columns].rearrange("m (u p e) -> m u p e", u=2, e=2),
+                        in0=result[:, columns].rearrange("m (p u e) -> m u p e", u=2, e=2),
+                        scalar1=1.0,
+                        scalar2=0.0,
+                        op0=mybir.AluOpType.mult,
+                        op1=mybir.AluOpType.add,
+                    )
+                nc.sync.dma_start(out=hop1_out[s][rows, :], in_=result[:])
 
         def second_hop(pair):
             s = pair % SUPPORTS
             for j in range(TILES):
-                row_tile, rows = rows_of(pair, j)
+                rows = rows_of(pair, j)[1]
                 codes, scales = hop1_q[TILES * pair + j]
-                hop(codes, scales, s, hop2_out[s][rows, :], None)
+                result = result_pool.tile([P, NODES], F32, name="result")
+                for half in range(HALVES):
+                    sums, columns = product(codes[:], scales[:], s, half)
+                    if half == 0:
+                        nc.scalar.copy(out=result[:, columns], in_=sums[:])
+                    else:
+                        nc.vector.tensor_copy(out=result[:, columns], in_=sums[:])
+                    nc.sync.dma_start(out=hop2_out[s][rows, columns], in_=result[:, columns])
 
         def flip_hop1(sorted_bf16):
             flipped = flip_pool.tile([P, BANK], F32, name="flipped")
@@ -192,47 +191,59 @@ def tile_adaptivegcn_pb_kernel(
                 nc.tensor.transpose(flipped[:, columns], planes[:, columns], identity[:])
             return flipped
 
-        def group_hop1(flipped, grouped):
+        def group_hop1(flipped):
+            grouped = grouped_pool.tile([P, TILE_VALUES], BF16, name="grouped", align_bytes=64)
             nc.vector.tensor_copy(
-                out=grouped.bitcast(F32).rearrange("p (g m u) -> p g m u", g=GROUPS, u=2),
+                out=grouped[:].bitcast(F32).rearrange("p (g m u) -> p g m u", g=GROUPS, u=2),
                 in_=flipped[:].rearrange("p (g u m) -> p g m u", g=GROUPS, u=2),
             )
+            return grouped
+
+        def quantise(grouped, codes, scales):
+            nc.vector.quantize_mx(out=codes.bitcast(FP8X4), scales=scales, in_=grouped[:])
+
+        def transposes(old_results, x_tiles, new_results):
+            sources = [("result", r) for r in old_results]
+            sources += [("x", row_tile) for row_tile in x_tiles]
+            sources += [("result", r) for r in new_results]
+            grouped_before = None
+            for kind, number in sources:
+                if kind == "x":
+                    grouped = group_x(flip_x(number))
+                    codes, scales = x_codes[:, number, :], x_scales[:, number, :]
+                else:
+                    grouped = group_hop1(flip_hop1(hop1_bf[number]))
+                    codes = hop1_q_pool.tile([P, TILE_WORDS], U32, name="codes", align_bytes=64)
+                    scales = hop1_q_pool.tile([P, TILE_WORDS], U8, name="scales", align_bytes=64)
+                    hop1_q[number] = (codes, scales)
+                if grouped_before is not None:
+                    quantise(*grouped_before)
+                grouped_before = (grouped, codes, scales)
+            quantise(*grouped_before)
 
         def x_tiles_of_step(n):
             if n < 2:
                 return [TILES * n, TILES * n + 1]
             return [row_tile for row_tile in [n + 2] if row_tile < ROW_TILES]
 
+        def results_of_step(n):
+            old = [r for r in [2 * n - 3] if 0 <= r]
+            new = [r for r in [2 * n - 2] if 0 <= r]
+            if n == PRODUCTS:
+                new.append(RESULTS - 1)
+            return old, new
+
         for row_tile in x_tiles_of_step(0):
             sort_x(row_tile)
         for row_tile in x_tiles_of_step(0):
-            quantise_x(row_tile, group_x(flip_x(row_tile)))
+            transposes([], [row_tile], [])
 
         for n in range(PRODUCTS + 2):
-            if n > 0:
-                x_tiles = x_tiles_of_step(n)
-                numbers = [r for r in (2 * n - 3, 2 * n - 2) if 0 <= r < TILES * PRODUCTS]
-                grouped_x = [group_x(flip_x(row_tile)) for row_tile in x_tiles]
-                grouped_h = grouped_pool.tile(
-                    [P, len(numbers) * TILE_VALUES], BF16, name="grouped_h", align_bytes=64
-                )
-                for place, r in enumerate(numbers):
-                    group_hop1(
-                        flip_hop1(hop1_bf[r]),
-                        grouped_h[:, place * TILE_VALUES : (place + 1) * TILE_VALUES],
-                    )
-                for row_tile, grouped in zip(x_tiles, grouped_x):
-                    quantise_x(row_tile, grouped)
-                codes = hop1_q_pool.tile([P, len(numbers) * TILE_WORDS], U32, name="codes", align_bytes=64)
-                scales = hop1_q_pool.tile([P, len(numbers) * TILE_WORDS], U8, name="scales", align_bytes=64)
-                nc.vector.quantize_mx(out=codes[:].bitcast(FP8X4), scales=scales[:], in_=grouped_h[:])
-                for place, r in enumerate(numbers):
-                    words = slice(place * TILE_WORDS, (place + 1) * TILE_WORDS)
-                    hop1_q[r] = (codes[:, words], scales[:, words])
-
+            if 1 <= n <= PRODUCTS:
+                old_results, new_results = results_of_step(n)
+                transposes(old_results, x_tiles_of_step(n), new_results)
             for row_tile in x_tiles_of_step(n + 1):
                 sort_x(row_tile)
-
             if n < PRODUCTS:
                 first_hop(n)
             if n >= 2:

@@ -97,8 +97,9 @@ def tile_adaptivegcn_pb_kernel(
             by_step = x_raw[:, b, :].rearrange(
                 "q (p u e l) -> q l u p e", u=2, e=2, l=STEPS_OF_TIME
             )
+            copy = nc.vector.tensor_copy if b < 2 else nc.scalar.copy
             for step_of_time in (2 * j, 2 * j + 1):
-                nc.vector.tensor_copy(
+                copy(
                     out=x_sorted[:, b, step_of_time * BANK : (step_of_time + 1) * BANK].rearrange(
                         "q (u p e) -> q u p e", u=2, e=2
                     ),

@@ -62,17 +62,20 @@ def tile_adaptivegcn_pb_kernel(
         x_raw = keep.tile([P, BLOCKS, BANK * STEPS_OF_TIME], BF16)
         x_view = x.rearrange("b c (g f) -> b (c g) f", g=GROUPS)
         w_words = keep.tile([P, SUPPORTS, GROUPS, NODES], U32, align_bytes=64)
-        w_scales = keep.tile([P, NODES], U8, align_bytes=64)
-        nc.vector.memset(w_scales[:].bitcast(I32), 0)
+        w_scales = []
+        for s in range(SUPPORTS):
+            planes = keep.tile([P, NODES], U8, name="w_scales_%d" % s, align_bytes=64)
+            nc.vector.memset(planes[:].bitcast(I32), 0)
+            w_scales.append(planes)
 
         def load_x(b):
             nc.sync.dma_start(out=x_raw[:, b, :], in_=x_view[b])
 
         def load_support(s):
             for quadrant in range(4):
-                first = 32 * quadrant + 8 * s
+                first = 32 * quadrant
                 nc.sync.dma_start(
-                    out=w_scales[first : first + 8, :].bitcast(I32),
+                    out=w_scales[s][first : first + 8, :].bitcast(I32),
                     in_=scales_in[s][:, 4 * quadrant : 4 * quadrant + 4, :].bitcast(I32),
                 )
             for g in range(GROUPS):
@@ -137,7 +140,7 @@ def tile_adaptivegcn_pb_kernel(
                     lhsT=codes[:, rows].bitcast(FP8X4),
                     lhsT_scale=scales[:, rows],
                     rhs=w_words[:, s, g, columns].bitcast(FP8X4),
-                    rhs_scale=w_scales[8 * s + 4 * g : P, columns],
+                    rhs_scale=w_scales[s][4 * g : P, columns],
                     start=(g == 0),
                     stop=(g == GROUPS - 1),
                 )

@@ -100,7 +100,7 @@ def tile_adaptivegcn_pb_kernel(
             by_step = x_raw[:, b, :].rearrange(
                 "q (p u e l) -> q l u p e", u=2, e=2, l=STEPS_OF_TIME
             )
-            copy = nc.vector.tensor_copy if b < 2 else nc.scalar.copy
+            copy = nc.scalar.copy if row_tile == 1 else nc.vector.tensor_copy
             for step_of_time in (2 * j, 2 * j + 1):
                 copy(
                     out=x_sorted[:, b, step_of_time * BANK : (step_of_time + 1) * BANK].rearrange(
@@ -230,12 +230,15 @@ def tile_adaptivegcn_pb_kernel(
                 return [TILES * n, TILES * n + 1]
             return [row_tile for row_tile in [n + 2] if row_tile < ROW_TILES]
 
+        last_step_with_x = ROW_TILES - 3
+
+        def transposed_by(n):
+            if n <= last_step_with_x:
+                return max(0, 2 * (n - 1))
+            return min(RESULTS, 2 * (last_step_with_x - 1) + 3 * (n - last_step_with_x))
+
         def results_of_step(n):
-            old = [r for r in [2 * n - 3] if 0 <= r]
-            new = [r for r in [2 * n - 2] if 0 <= r]
-            if n == PRODUCTS:
-                new.append(RESULTS - 1)
-            return old, new
+            return list(range(transposed_by(n - 1), transposed_by(n))), []
 
         for row_tile in x_tiles_of_step(0):
             sort_x(row_tile)

@@ -25,6 +25,9 @@ TILE_VALUES = 4 * TILE_WORDS
 PRODUCTS = BLOCKS * SUPPORTS
 RESULTS = TILES * PRODUCTS
 
+WARM_BEFORE_X = 6
+WARM_BEFORE_PASSES = 2
+
 FLOPS = 2 * 2 * SUPPORTS * 1024 * NODES * NODES
 
 
@@ -91,6 +94,16 @@ def tile_adaptivegcn_pb_kernel(
         load_x(2)
         load_x(3)
 
+        zeros = keep.tile([P, BANK], BF16, name="zeros")
+        nc.vector.memset(zeros[:], 0.0)
+
+        def idle_matmuls(count):
+            unread = sum_pool.tile([P, BANK], F32, name="sums")
+            for i in range(count):
+                nc.tensor.matmul(out=unread[:], lhsT=zeros[:, :P], rhs=zeros[:], start=True, stop=True)
+
+        idle_matmuls(WARM_BEFORE_X)
+
         x_sorted = keep.tile([P, BLOCKS, STEPS_OF_TIME * BANK], BF16)
         x_codes = keep.tile([P, ROW_TILES, TILE_WORDS], U32, align_bytes=64)
         x_scales = keep.tile([P, ROW_TILES, TILE_WORDS], U8, align_bytes=64)
@@ -111,23 +124,31 @@ def tile_adaptivegcn_pb_kernel(
 
         def flip_x(row_tile):
             b, j = divmod(row_tile, TILES)
-            flipped = flip_pool.tile([P, BANK], F32, name="flipped")
             planes = x_sorted[:, b, :].bitcast(F32)
-            for plane in range(4):
-                source = 4 * j + plane
-                nc.tensor.transpose(
-                    flipped[:, plane * P : (plane + 1) * P],
-                    planes[:, source * P : (source + 1) * P],
-                    identity[:],
-                )
-            return flipped
+            banks = 2 if row_tile == 0 else 1
+            views = []
+            for step in range(2):
+                if step % (2 // banks) == 0:
+                    flipped = flip_pool.tile([P, BANK], F32, name="flipped")
+                first = (step % (2 // banks)) * 2 * P
+                for u in range(2):
+                    source = 4 * j + 2 * step + u
+                    nc.tensor.transpose(
+                        flipped[:, first + u * P : first + (u + 1) * P],
+                        planes[:, source * P : (source + 1) * P],
+                        identity[:],
+                    )
+                views.append(flipped[:, first : first + 2 * P])
+            return views
 
-        def group_x(flipped):
+        def group_x(views):
             grouped = grouped_pool.tile([P, TILE_VALUES], BF16, name="grouped", align_bytes=64)
-            by_group = flipped[:].rearrange("p (l u c g) -> p g l c u", l=2, u=2, g=GROUPS)
-            pairs = grouped[:].bitcast(F32).rearrange("p (g l c u) -> p g l c u", g=GROUPS, l=2, u=2)
-            for g in range(GROUPS):
-                nc.vector.tensor_copy(out=pairs[:, g], in_=by_group[:, g])
+            pairs = grouped[:].bitcast(F32).rearrange("p (g l c u) -> p l g c u", g=GROUPS, l=2, u=2)
+            for step in range(2):
+                nc.vector.tensor_copy(
+                    out=pairs[:, step],
+                    in_=views[step].rearrange("p (u c g) -> p g c u", u=2, g=GROUPS),
+                )
             return grouped
 
         def product(codes, scales, s, half):
@@ -244,6 +265,7 @@ def tile_adaptivegcn_pb_kernel(
             sort_x(row_tile)
         for row_tile in x_tiles_of_step(0):
             transposes([], [row_tile], [])
+        idle_matmuls(WARM_BEFORE_PASSES)
 
         for n in range(PRODUCTS + 2):
             if 1 <= n <= PRODUCTS:

@@ -81,11 +81,14 @@ def tile_adaptivegcn_pb_kernel(
                     out=w_scales[s][first : first + 8, :].bitcast(I32),
                     in_=scales_in[s][:, 4 * quadrant : 4 * quadrant + 4, :].bitcast(I32),
                 )
-            for g in range(GROUPS):
-                nc.sync.dma_start(
-                    out=w_words[:, s, g, :].bitcast(I32),
-                    in_=words_in[s][g].rearrange("p n t -> p (n t)").bitcast(I32),
-                )
+            for half in range(HALVES):
+                for g in range(GROUPS):
+                    nc.sync.dma_start(
+                        out=w_words[:, s, g, half * BANK : (half + 1) * BANK].bitcast(I32),
+                        in_=words_in[s][g, :, half * BANK : (half + 1) * BANK, :]
+                        .rearrange("p n t -> p (n t)")
+                        .bitcast(I32),
+                    )
 
         load_x(0)
         load_support(0)

@@ -172,10 +172,16 @@ def tile_adaptivegcn_pb_kernel(
 
         hop1_bf = {}
         hop1_q = {}
+        last_codes = []
 
         def rows_of(pair, j):
             row_tile = (pair // SUPPORTS) * TILES + j
             return row_tile, slice(row_tile * P, (row_tile + 1) * P)
+
+        gates = keep.tile([P, PRODUCTS], U32, name="gates")
+
+        def hold_gpsimd(step):
+            nc.gpsimd.tensor_copy(out=gates[:, step : step + 1], in_=last_codes[-1][:, :1])
 
         def first_hop(pair):
             s = pair % SUPPORTS
@@ -229,6 +235,7 @@ def tile_adaptivegcn_pb_kernel(
 
         def quantise(grouped, codes, scales):
             nc.vector.quantize_mx(out=codes.bitcast(FP8X4), scales=scales, in_=grouped[:])
+            last_codes.append(codes)
 
         def transposes(old_results, x_tiles, new_results):
             sources = [("result", r) for r in old_results]
@@ -276,6 +283,8 @@ def tile_adaptivegcn_pb_kernel(
                 transposes(old_results, x_tiles_of_step(n), new_results)
             for row_tile in x_tiles_of_step(n + 1):
                 sort_x(row_tile)
+            if 1 <= n <= last_step_with_x:
+                hold_gpsimd(n)
             if n < PRODUCTS:
                 first_hop(n)
             if n >= 2:

@@ -25,8 +25,8 @@ TILE_VALUES = 4 * TILE_WORDS
 PRODUCTS = BLOCKS * SUPPORTS
 RESULTS = TILES * PRODUCTS
 
-WARM_BEFORE_X = 6
-WARM_BEFORE_PASSES = 2
+WARM_BEFORE_X = 3
+WARM_BEFORE_PASSES = 1
 
 FLOPS = 2 * 2 * SUPPORTS * 1024 * NODES * NODES
 
@@ -71,8 +71,14 @@ def tile_adaptivegcn_pb_kernel(
             nc.vector.memset(planes[:].bitcast(I32), 0)
             w_scales.append(planes)
 
+        def x_pieces(b):
+            return 2 if b < 2 else 1
+
         def load_x(b):
-            nc.sync.dma_start(out=x_raw[:, b, :], in_=x_view[b])
+            width = BANK * STEPS_OF_TIME // x_pieces(b)
+            for piece in range(x_pieces(b)):
+                elements = slice(piece * width, (piece + 1) * width)
+                nc.sync.dma_start(out=x_raw[:, b, elements], in_=x_view[b][:, elements])
 
         def load_support(s):
             for quadrant in range(4):
@@ -111,18 +117,25 @@ def tile_adaptivegcn_pb_kernel(
         x_codes = keep.tile([P, ROW_TILES, TILE_WORDS], U32, align_bytes=64)
         x_scales = keep.tile([P, ROW_TILES, TILE_WORDS], U8, align_bytes=64)
 
-        def sort_x(row_tile):
-            b, j = divmod(row_tile, TILES)
+        def sort_x(row_tiles):
+            for piece in range(2):
+                for row_tile in row_tiles:
+                    b, j = divmod(row_tile, TILES)
+                    if piece < x_pieces(b):
+                        sort_piece(row_tile, b, j, piece)
+
+        def sort_piece(row_tile, b, j, piece):
             by_step = x_raw[:, b, :].rearrange(
                 "q (p u e l) -> q l u p e", u=2, e=2, l=STEPS_OF_TIME
             )
             copy = nc.scalar.copy if row_tile == 1 else nc.vector.tensor_copy
+            width = P // x_pieces(b)
+            places = slice(piece * width, (piece + 1) * width)
             for step_of_time in (2 * j, 2 * j + 1):
+                sorted_step = x_sorted[:, b, step_of_time * BANK : (step_of_time + 1) * BANK]
                 copy(
-                    out=x_sorted[:, b, step_of_time * BANK : (step_of_time + 1) * BANK].rearrange(
-                        "q (u p e) -> q u p e", u=2, e=2
-                    ),
-                    in_=by_step[:, step_of_time],
+                    out=sorted_step.rearrange("q (u p e) -> q u p e", u=2, e=2)[:, :, places, :],
+                    in_=by_step[:, step_of_time, :, places, :],
                 )
 
         def flip_x(row_tile):
@@ -144,23 +157,24 @@ def tile_adaptivegcn_pb_kernel(
                 views.append(flipped[:, first : first + 2 * P])
             return views
 
-        def group_x(views):
+        def group_x(row_tile, views):
             grouped = grouped_pool.tile([P, TILE_VALUES], BF16, name="grouped", align_bytes=64)
             pairs = grouped[:].bitcast(F32).rearrange("p (g l c u) -> p l g c u", g=GROUPS, l=2, u=2)
             for step in range(2):
-                nc.vector.tensor_copy(
+                copy = nc.scalar.copy if (row_tile, step) == (0, 1) else nc.vector.tensor_copy
+                copy(
                     out=pairs[:, step],
                     in_=views[step].rearrange("p (u c g) -> p g c u", u=2, g=GROUPS),
                 )
             return grouped
 
-        def product(codes, scales, s, half):
-            columns = slice(half * BANK, (half + 1) * BANK)
-            sums = sum_pool.tile([P, BANK], F32, name="sums")
+        def product(codes, scales, s, columns):
+            bank = sum_pool.tile([P, BANK], F32, name="sums")
+            sums = bank[:, : columns.stop - columns.start]
             for g in range(GROUPS):
                 rows = slice(g * P, (g + 1) * P)
                 nc.tensor.matmul_mx(
-                    out=sums[:],
+                    out=sums,
                     lhsT=codes[:, rows].bitcast(FP8X4),
                     lhsT_scale=scales[:, rows],
                     rhs=w_words[:, s, g, columns].bitcast(FP8X4),
@@ -168,7 +182,10 @@ def tile_adaptivegcn_pb_kernel(
                     start=(g == 0),
                     stop=(g == GROUPS - 1),
                 )
-            return sums, columns
+            return sums
+
+        def half_columns(half):
+            return slice(half * BANK, (half + 1) * BANK)
 
         hop1_bf = {}
         hop1_q = {}
@@ -185,37 +202,49 @@ def tile_adaptivegcn_pb_kernel(
 
         def first_hop(pair):
             s = pair % SUPPORTS
+            results = []
             for j in range(TILES):
-                row_tile, rows = rows_of(pair, j)
                 result = result_pool.tile([P, NODES], F32, name="result")
+                results.append(result)
                 sorted_bf16 = hop1_bf_pool.tile([P, NODES], BF16, name="sorted_bf16")
                 hop1_bf[TILES * pair + j] = sorted_bf16
-                for half in range(HALVES):
-                    sums, columns = product(x_codes[:, row_tile, :], x_scales[:, row_tile, :], s, half)
-                    nc.scalar.copy(out=result[:, columns], in_=sums[:])
-                    nc.gpsimd.tensor_scalar(
-                        out=sorted_bf16[:, columns].rearrange("m (u p e) -> m u p e", u=2, e=2),
-                        in0=result[:, columns].rearrange("m (p u e) -> m u p e", u=2, e=2),
-                        scalar1=1.0,
-                        scalar2=0.0,
-                        op0=mybir.AluOpType.mult,
-                        op1=mybir.AluOpType.add,
-                    )
-                nc.sync.dma_start(out=hop1_out[s][rows, :], in_=result[:])
+            if pair in (1,):
+                order = [(j, half) for half in range(HALVES) for j in range(TILES)]
+            else:
+                order = [(j, half) for j in range(TILES) for half in range(HALVES)]
+            for j, half in order:
+                row_tile, rows = rows_of(pair, j)
+                result, sorted_bf16 = results[j], hop1_bf[TILES * pair + j]
+                columns = half_columns(half)
+                sums = product(x_codes[:, row_tile, :], x_scales[:, row_tile, :], s, columns)
+                nc.scalar.copy(out=result[:, columns], in_=sums)
+                nc.gpsimd.tensor_scalar(
+                    out=sorted_bf16[:, columns].rearrange("m (u p e) -> m u p e", u=2, e=2),
+                    in0=result[:, columns].rearrange("m (p u e) -> m u p e", u=2, e=2),
+                    scalar1=1.0,
+                    scalar2=0.0,
+                    op0=mybir.AluOpType.mult,
+                    op1=mybir.AluOpType.add,
+                )
+                if pair == PRODUCTS - 1:
+                    nc.sync.dma_start(out=hop1_out[s][rows, columns], in_=result[:, columns])
+                elif half == HALVES - 1:
+                    nc.sync.dma_start(out=hop1_out[s][rows, :], in_=result[:])
 
-        def second_hop(pair):
+        def second_hop(number):
+            pair, j = divmod(number, TILES)
             s = pair % SUPPORTS
-            for j in range(TILES):
-                rows = rows_of(pair, j)[1]
-                codes, scales = hop1_q[TILES * pair + j]
-                result = result_pool.tile([P, NODES], F32, name="result")
-                for half in range(HALVES):
-                    sums, columns = product(codes[:], scales[:], s, half)
-                    if half == 0:
-                        nc.scalar.copy(out=result[:, columns], in_=sums[:])
-                    else:
-                        nc.vector.tensor_copy(out=result[:, columns], in_=sums[:])
-                    nc.sync.dma_start(out=hop2_out[s][rows, columns], in_=result[:, columns])
+            rows = rows_of(pair, j)[1]
+            codes, scales = hop1_q[number]
+            result = result_pool.tile([P, NODES], F32, name="result")
+            for half in range(HALVES):
+                columns = half_columns(half)
+                sums = product(codes[:], scales[:], s, columns)
+                if half == 0:
+                    nc.scalar.copy(out=result[:, columns], in_=sums)
+                else:
+                    nc.vector.tensor_copy(out=result[:, columns], in_=sums)
+                nc.sync.dma_start(out=hop2_out[s][rows, columns], in_=result[:, columns])
 
         def flip_hop1(sorted_bf16):
             flipped = flip_pool.tile([P, BANK], F32, name="flipped")
@@ -244,7 +273,7 @@ def tile_adaptivegcn_pb_kernel(
             grouped_before = None
             for kind, number in sources:
                 if kind == "x":
-                    grouped = group_x(flip_x(number))
+                    grouped = group_x(number, flip_x(number))
                     codes, scales = x_codes[:, number, :], x_scales[:, number, :]
                 else:
                     grouped = group_hop1(flip_hop1(hop1_bf[number]))
@@ -271,21 +300,25 @@ def tile_adaptivegcn_pb_kernel(
         def results_of_step(n):
             return list(range(transposed_by(n - 1), transposed_by(n))), []
 
-        for row_tile in x_tiles_of_step(0):
-            sort_x(row_tile)
-        for row_tile in x_tiles_of_step(0):
-            transposes([], [row_tile], [])
+        sort_x(x_tiles_of_step(0))
+        transposes([], [0], [])
         idle_matmuls(WARM_BEFORE_PASSES)
+        transposes([], [1], [])
 
-        for n in range(PRODUCTS + 2):
-            if 1 <= n <= PRODUCTS:
+        for n in range(PRODUCTS):
+            if n >= 1:
                 old_results, new_results = results_of_step(n)
                 transposes(old_results, x_tiles_of_step(n), new_results)
-            for row_tile in x_tiles_of_step(n + 1):
-                sort_x(row_tile)
+            sort_x(x_tiles_of_step(n + 1))
             if 1 <= n <= last_step_with_x:
                 hold_gpsimd(n)
-            if n < PRODUCTS:
-                first_hop(n)
+            first_hop(n)
             if n >= 2:
-                second_hop(n - 2)
+                for j in range(TILES):
+                    second_hop(TILES * (n - 2) + j)
+        transposes([14], [], [])
+        second_hop(12)
+        transposes([15], [], [])
+        second_hop(13)
+        second_hop(14)
+        second_hop(15)

from contextlib import ExitStack

import concourse.mybir as mybir
from concourse.masks import make_identity

F32 = mybir.dt.float32
BF16 = mybir.dt.bfloat16
I32 = mybir.dt.int32
U32 = mybir.dt.uint32
U8 = mybir.dt.uint8
FP8X4 = mybir.dt.float8_e4m3fn_x4

P = 128
NODES = 1024
GROUPS = 2
BANK = 512
HALVES = NODES // BANK
BLOCKS = 4
TILES = 2
ROW_TILES = BLOCKS * TILES
STEPS_OF_TIME = 4
SUPPORTS = 2
TILE_WORDS = GROUPS * P
TILE_VALUES = 4 * TILE_WORDS
PRODUCTS = BLOCKS * SUPPORTS
RESULTS = TILES * PRODUCTS

WARM_BEFORE_X = 3
WARM_BEFORE_PASSES = 1

FLOPS = 2 * 2 * SUPPORTS * 1024 * NODES * NODES


def tile_adaptivegcn_pb_kernel(
    tc,
    x,
    support0_words,
    support0_scales,
    support1_words,
    support1_scales,
    out_0,
    out_1,
    out_2,
    out_3,
):
    nc = tc.nc
    words_in = [support0_words, support1_words]
    scales_in = [support0_scales, support1_scales]
    hop1_out = [out_0.flatten_outer_dims(), out_2.flatten_outer_dims()]
    hop2_out = [out_1.flatten_outer_dims(), out_3.flatten_outer_dims()]

    with ExitStack() as ctx:
        ctx.enter_context(tc.manual_schedule())
        keep = ctx.enter_context(tc.tile_pool(name="keep", bufs=1))
        grouped_pool = ctx.enter_context(tc.tile_pool(name="grouped", bufs=4))
        hop1_q_pool = ctx.enter_context(tc.tile_pool(name="hop1_q", bufs=6))
        hop1_bf_pool = ctx.enter_context(tc.tile_pool(name="hop1_bf", bufs=6))
        result_pool = ctx.enter_context(tc.tile_pool(name="result", bufs=12))
        sum_pool = ctx.enter_context(tc.psum_pool(name="sums", bufs=5))
        flip_pool = ctx.enter_context(tc.psum_pool(name="flips", bufs=3))

        identity = keep.tile([P, P], F32)
        make_identity(nc, identity[:])

        x_raw = keep.tile([P, BLOCKS, BANK * STEPS_OF_TIME], BF16)
        x_view = x.rearrange("b c (g f) -> b (c g) f", g=GROUPS)
        w_words = keep.tile([P, SUPPORTS, GROUPS, NODES], U32, align_bytes=64)
        w_scales = []
        for s in range(SUPPORTS):
            planes = keep.tile([P, NODES], U8, name="w_scales_%d" % s, align_bytes=64)
            nc.vector.memset(planes[:].bitcast(I32), 0)
            w_scales.append(planes)

        def x_pieces(b):
            return 2 if b < 2 else 1

        def load_x(b):
            width = BANK * STEPS_OF_TIME // x_pieces(b)
            for piece in range(x_pieces(b)):
                elements = slice(piece * width, (piece + 1) * width)
                nc.sync.dma_start(out=x_raw[:, b, elements], in_=x_view[b][:, elements])

        def load_support(s):
            for quadrant in range(4):
                first = 32 * quadrant
                nc.sync.dma_start(
                    out=w_scales[s][first : first + 8, :].bitcast(I32),
                    in_=scales_in[s][:, 4 * quadrant : 4 * quadrant + 4, :].bitcast(I32),
                )
            for half in range(HALVES):
                for g in range(GROUPS):
                    nc.sync.dma_start(
                        out=w_words[:, s, g, half * BANK : (half + 1) * BANK].bitcast(I32),
                        in_=words_in[s][g, :, half * BANK : (half + 1) * BANK, :]
                        .rearrange("p n t -> p (n t)")
                        .bitcast(I32),
                    )

        load_x(0)
        load_support(0)
        load_x(1)
        load_support(1)
        load_x(2)
        load_x(3)

        zeros = keep.tile([P, BANK], BF16, name="zeros")
        nc.vector.memset(zeros[:], 0.0)

        def idle_matmuls(count):
            unread = sum_pool.tile([P, BANK], F32, name="sums")
            for i in range(count):
                nc.tensor.matmul(out=unread[:], lhsT=zeros[:, :P], rhs=zeros[:], start=True, stop=True)

        idle_matmuls(WARM_BEFORE_X)

        x_sorted = keep.tile([P, BLOCKS, STEPS_OF_TIME * BANK], BF16)
        x_codes = keep.tile([P, ROW_TILES, TILE_WORDS], U32, align_bytes=64)
        x_scales = keep.tile([P, ROW_TILES, TILE_WORDS], U8, align_bytes=64)

        def sort_x(row_tiles):
            for piece in range(2):
                for row_tile in row_tiles:
                    b, j = divmod(row_tile, TILES)
                    if piece < x_pieces(b):
                        sort_piece(row_tile, b, j, piece)

        def sort_piece(row_tile, b, j, piece):
            by_step = x_raw[:, b, :].rearrange(
                "q (p u e l) -> q l u p e", u=2, e=2, l=STEPS_OF_TIME
            )
            copy = nc.scalar.copy if row_tile == 1 else nc.vector.tensor_copy
            width = P // x_pieces(b)
            places = slice(piece * width, (piece + 1) * width)
            for step_of_time in (2 * j, 2 * j + 1):
                sorted_step = x_sorted[:, b, step_of_time * BANK : (step_of_time + 1) * BANK]
                copy(
                    out=sorted_step.rearrange("q (u p e) -> q u p e", u=2, e=2)[:, :, places, :],
                    in_=by_step[:, step_of_time, :, places, :],
                )

        def flip_x(row_tile):
            b, j = divmod(row_tile, TILES)
            planes = x_sorted[:, b, :].bitcast(F32)
            banks = 2 if row_tile == 0 else 1
            views = []
            for step in range(2):
                if step % (2 // banks) == 0:
                    flipped = flip_pool.tile([P, BANK], F32, name="flipped")
                first = (step % (2 // banks)) * 2 * P
                for u in range(2):
                    source = 4 * j + 2 * step + u
                    nc.tensor.transpose(
                        flipped[:, first + u * P : first + (u + 1) * P],
                        planes[:, source * P : (source + 1) * P],
                        identity[:],
                    )
                views.append(flipped[:, first : first + 2 * P])
            return views

        def group_x(row_tile, views):
            grouped = grouped_pool.tile([P, TILE_VALUES], BF16, name="grouped", align_bytes=64)
            pairs = grouped[:].bitcast(F32).rearrange("p (g l c u) -> p l g c u", g=GROUPS, l=2, u=2)
            for step in range(2):
                copy = nc.scalar.copy if (row_tile, step) == (0, 1) else nc.vector.tensor_copy
                copy(
                    out=pairs[:, step],
                    in_=views[step].rearrange("p (u c g) -> p g c u", u=2, g=GROUPS),
                )
            return grouped

        def product(codes, scales, s, columns):
            bank = sum_pool.tile([P, BANK], F32, name="sums")
            sums = bank[:, : columns.stop - columns.start]
            for g in range(GROUPS):
                rows = slice(g * P, (g + 1) * P)
                nc.tensor.matmul_mx(
                    out=sums,
                    lhsT=codes[:, rows].bitcast(FP8X4),
                    lhsT_scale=scales[:, rows],
                    rhs=w_words[:, s, g, columns].bitcast(FP8X4),
                    rhs_scale=w_scales[s][4 * g : P, columns],
                    start=(g == 0),
                    stop=(g == GROUPS - 1),
                )
            return sums

        def half_columns(half):
            return slice(half * BANK, (half + 1) * BANK)

        hop1_bf = {}
        hop1_q = {}
        last_codes = []

        def rows_of(pair, j):
            row_tile = (pair // SUPPORTS) * TILES + j
            return row_tile, slice(row_tile * P, (row_tile + 1) * P)

        gates = keep.tile([P, PRODUCTS], U32, name="gates")

        def hold_gpsimd(step):
            nc.gpsimd.tensor_copy(out=gates[:, step : step + 1], in_=last_codes[-1][:, :1])

        def first_hop(pair):
            s = pair % SUPPORTS
            results = []
            for j in range(TILES):
                result = result_pool.tile([P, NODES], F32, name="result")
                results.append(result)
                sorted_bf16 = hop1_bf_pool.tile([P, NODES], BF16, name="sorted_bf16")
                hop1_bf[TILES * pair + j] = sorted_bf16
            if pair in (1,):
                order = [(j, half) for half in range(HALVES) for j in range(TILES)]
            else:
                order = [(j, half) for j in range(TILES) for half in range(HALVES)]
            for j, half in order:
                row_tile, rows = rows_of(pair, j)
                result, sorted_bf16 = results[j], hop1_bf[TILES * pair + j]
                columns = half_columns(half)
                sums = product(x_codes[:, row_tile, :], x_scales[:, row_tile, :], s, columns)
                nc.scalar.copy(out=result[:, columns], in_=sums)
                nc.gpsimd.tensor_scalar(
                    out=sorted_bf16[:, columns].rearrange("m (u p e) -> m u p e", u=2, e=2),
                    in0=result[:, columns].rearrange("m (p u e) -> m u p e", u=2, e=2),
                    scalar1=1.0,
                    scalar2=0.0,
                    op0=mybir.AluOpType.mult,
                    op1=mybir.AluOpType.add,
                )
                if pair == PRODUCTS - 1:
                    nc.sync.dma_start(out=hop1_out[s][rows, columns], in_=result[:, columns])
                elif half == HALVES - 1:
                    nc.sync.dma_start(out=hop1_out[s][rows, :], in_=result[:])

        def second_hop(number):
            pair, j = divmod(number, TILES)
            s = pair % SUPPORTS
            rows = rows_of(pair, j)[1]
            codes, scales = hop1_q[number]
            result = result_pool.tile([P, NODES], F32, name="result")
            for half in range(HALVES):
                columns = half_columns(half)
                sums = product(codes[:], scales[:], s, columns)
                if half == 0:
                    nc.scalar.copy(out=result[:, columns], in_=sums)
                else:
                    nc.vector.tensor_copy(out=result[:, columns], in_=sums)
                nc.sync.dma_start(out=hop2_out[s][rows, columns], in_=result[:, columns])

        def flip_hop1(sorted_bf16):
            flipped = flip_pool.tile([P, BANK], F32, name="flipped")
            planes = sorted_bf16[:].bitcast(F32)
            for plane in range(4):
                columns = slice(plane * P, (plane + 1) * P)
                nc.tensor.transpose(flipped[:, columns], planes[:, columns], identity[:])
            return flipped

        def group_hop1(flipped):
            grouped = grouped_pool.tile([P, TILE_VALUES], BF16, name="grouped", align_bytes=64)
            nc.vector.tensor_copy(
                out=grouped[:].bitcast(F32).rearrange("p (g m u) -> p g m u", g=GROUPS, u=2),
                in_=flipped[:].rearrange("p (g u m) -> p g m u", g=GROUPS, u=2),
            )
            return grouped

        def quantise(grouped, codes, scales):
            nc.vector.quantize_mx(out=codes.bitcast(FP8X4), scales=scales, in_=grouped[:])
            last_codes.append(codes)

        def transposes(old_results, x_tiles, new_results):
            sources = [("result", r) for r in old_results]
            sources += [("x", row_tile) for row_tile in x_tiles]
            sources += [("result", r) for r in new_results]
            grouped_before = None
            for kind, number in sources:
                if kind == "x":
                    grouped = group_x(number, flip_x(number))
                    codes, scales = x_codes[:, number, :], x_scales[:, number, :]
                else:
                    grouped = group_hop1(flip_hop1(hop1_bf[number]))
                    codes = hop1_q_pool.tile([P, TILE_WORDS], U32, name="codes", align_bytes=64)
                    scales = hop1_q_pool.tile([P, TILE_WORDS], U8, name="scales", align_bytes=64)
                    hop1_q[number] = (codes, scales)
                if grouped_before is not None:
                    quantise(*grouped_before)
                grouped_before = (grouped, codes, scales)
            quantise(*grouped_before)

        def x_tiles_of_step(n):
            if n < 2:
                return [TILES * n, TILES * n + 1]
            return [row_tile for row_tile in [n + 2] if row_tile < ROW_TILES]

        last_step_with_x = ROW_TILES - 3

        def transposed_by(n):
            if n <= last_step_with_x:
                return max(0, 2 * (n - 1))
            return min(RESULTS, 2 * (last_step_with_x - 1) + 3 * (n - last_step_with_x))

        def results_of_step(n):
            return list(range(transposed_by(n - 1), transposed_by(n))), []

        sort_x(x_tiles_of_step(0))
        transposes([], [0], [])
        idle_matmuls(WARM_BEFORE_PASSES)
        transposes([], [1], [])

        for n in range(PRODUCTS):
            if n >= 1:
                old_results, new_results = results_of_step(n)
                transposes(old_results, x_tiles_of_step(n), new_results)
            sort_x(x_tiles_of_step(n + 1))
            if 1 <= n <= last_step_with_x:
                hold_gpsimd(n)
            first_hop(n)
            if n >= 2:
                for j in range(TILES):
                    second_hop(TILES * (n - 2) + j)
        transposes([14], [], [])
        second_hop(12)
        transposes([15], [], [])
        second_hop(13)
        second_hop(14)
        second_hop(15)
